import numpy as np
import ml_dtypes

BF16 = ml_dtypes.bfloat16


def bf(x):
    return np.asarray(x, np.float32).astype(BF16)


def f32(x):
    return np.asarray(x, np.float32)


def f64(x):
    return np.asarray(x).astype(np.float64)


def striped(idx):
    return np.tile(idx.reshape(-1, 16).T, (8, 1))


C, S, N = 256, 1024, 256


def setup_inputs():
    return {
        "base": f32(np.random.standard_normal((C, S))),
        "fs": bf(np.random.standard_normal((C, N))),
        "w_v": bf(np.random.standard_normal((C, C)) / np.sqrt(C)),
        "b_v": f32(0.1 * np.random.standard_normal((C, 1))),
        "w_o": bf(np.random.standard_normal((C, C)) / np.sqrt(C)),
        "b_o": f32(0.1 * np.random.standard_normal((C, 1))),
        "offs": striped(np.random.permutation(S)[:N]),
    }


def reference(base, fs, w_v, b_v, w_o, b_o, offs):
    idx = offs[:16].T.reshape(-1)
    v = f64(w_v).T @ f64(fs) + f64(b_v)
    s2 = f64(w_o).T @ v + f64(b_o)
    res = f64(base).copy()
    res[:, idx] = f64(fs) + s2
    return res

@@ -1,0 +1,71 @@
+import concourse.mybir as mybir
+
+P = 128
+C, S, N = 256, 1024, 256
+BLOCKS = C // P
+FLOPS = 2 * (2 * C * C * N)
+
+BF16, F32, U16 = mybir.dt.bfloat16, mybir.dt.float32, mybir.dt.uint16
+ADD = mybir.AluOpType.add
+IDENTITY = mybir.ActivationFunctionType.Identity
+
+
+def by_block(matrix):
+    return matrix.rearrange("(t p) n -> p t n", p=P)
+
+
+def tile_dsvt_ort_kernel(tc, base, fs, w_v, b_v, w_o, b_o, offs, out):
+    nc = tc.nc
+    with (
+        tc.tile_pool(name="held", bufs=1) as held,
+        tc.psum_pool(name="psum", bufs=1) as psum,
+    ):
+        offsets = held.tile([P, N // 16], U16, name="offsets")
+        nc.sync.dma_start(offsets[:], offs)
+
+        fs_bf = held.tile([P, BLOCKS, N], BF16, name="fs_bf")
+        wv_bf = held.tile([P, BLOCKS, C], BF16, name="wv_bf")
+        wo_bf = held.tile([P, BLOCKS, C], BF16, name="wo_bf")
+        nc.sync.dma_start(fs_bf[:], by_block(fs))
+        nc.scalar.dma_start(wv_bf[:], by_block(w_v))
+        nc.sync.dma_start(wo_bf[:], by_block(w_o))
+
+        bv = held.tile([P, BLOCKS], F32, name="bv")
+        bo = held.tile([P, BLOCKS], F32, name="bo")
+        with nc.allow_non_contiguous_dma(reason="a bias: one float32 for each partition and block"):
+            nc.scalar.dma_start(bv[:], b_v.rearrange("(t p) one -> p (t one)", p=P))
+            nc.scalar.dma_start(bo[:], b_o.rearrange("(t p) one -> p (t one)", p=P))
+
+        windows = [held.tile([P, S], F32, name=f"window{t}") for t in range(BLOCKS)]
+        nc.sync.dma_start(windows[0][:], base[0:P, :])
+        nc.scalar.dma_start(windows[1][:], base[P : 2 * P, :])
+
+        fs_f32 = [held.tile([P, N], F32, name=f"fs_f32_{t}") for t in range(BLOCKS)]
+        for t in range(BLOCKS):
+            nc.gpsimd.tensor_copy(fs_f32[t][:], fs_bf[:, t, :])
+
+        v_bf = [held.tile([P, N], BF16, name=f"v_bf{m}") for m in range(BLOCKS)]
+        for m in range(BLOCKS):
+            v_acc = psum.tile([P, N], F32, name=f"v_acc{m}")
+            for k in range(BLOCKS):
+                nc.tensor.matmul(
+                    v_acc[:], wv_bf[:, k, m * P : (m + 1) * P], fs_bf[:, k, :],
+                    start=(k == 0), stop=(k == BLOCKS - 1),
+                )
+            if m == 0:
+                nc.vector.tensor_scalar(v_bf[m][:], v_acc[:], bv[:, m : m + 1], None, ADD)
+            else:
+                nc.scalar.activation(v_bf[m][:], v_acc[:], IDENTITY, bias=bv[:, m : m + 1])
+
+        for c in range(BLOCKS):
+            s2_acc = psum.tile([P, N], F32, name=f"s2_acc{c}")
+            for m in range(BLOCKS):
+                nc.tensor.matmul(
+                    s2_acc[:], wo_bf[:, m, c * P : (c + 1) * P], v_bf[m][:],
+                    start=(m == 0), stop=(m == BLOCKS - 1),
+                )
+            s2 = held.tile([P, N], F32, name=f"s2_{c}")
+            nc.scalar.activation(s2[:], s2_acc[:], IDENTITY, bias=bo[:, c : c + 1])
+            nc.vector.tensor_tensor(windows[c][:].indirect(offsets[:]), fs_f32[c][:], s2[:], ADD)
+            store_queue = nc.sync if c == 0 else nc.scalar
+            store_queue.dma_start(out[c * P : (c + 1) * P, :], windows[c][:])

@@ -20,24 +20,27 @@ def tile_dsvt_ort_kernel(tc, base, fs, w_v, b_v, w_o, b_o, offs, out):
         tc.tile_pool(name="held", bufs=1) as held,
         tc.psum_pool(name="psum", bufs=1) as psum,
     ):
-        offsets = held.tile([P, N // 16], U16, name="offsets")
-        nc.sync.dma_start(offsets[:], offs)
-
         fs_bf = held.tile([P, BLOCKS, N], BF16, name="fs_bf")
         wv_bf = held.tile([P, BLOCKS, C], BF16, name="wv_bf")
         wo_bf = held.tile([P, BLOCKS, C], BF16, name="wo_bf")
-        nc.sync.dma_start(fs_bf[:], by_block(fs))
-        nc.scalar.dma_start(wv_bf[:], by_block(w_v))
-        nc.sync.dma_start(wo_bf[:], by_block(w_o))
-
         bv = held.tile([P, BLOCKS], F32, name="bv")
         bo = held.tile([P, BLOCKS], F32, name="bo")
-        with nc.allow_non_contiguous_dma(reason="a bias: one float32 for each partition and block"):
-            nc.scalar.dma_start(bv[:], b_v.rearrange("(t p) one -> p (t one)", p=P))
-            nc.scalar.dma_start(bo[:], b_o.rearrange("(t p) one -> p (t one)", p=P))
-
+        offsets = held.tile([P, N // 16], U16, name="offsets")
         windows = [held.tile([P, S], F32, name=f"window{t}") for t in range(BLOCKS)]
+
+        nc.sync.dma_start(fs_bf[:], by_block(fs))
+        nc.sync.dma_start(wv_bf[:], by_block(w_v))
+        with nc.allow_non_contiguous_dma(reason="a bias: one float32 for each partition and block"):
+            nc.sync.dma_start(bv[:], b_v.rearrange("(t p) one -> p (t one)", p=P))
+            nc.sync.dma_start(wo_bf[:], by_block(w_o))
+            nc.sync.dma_start(bo[:], b_o.rearrange("(t p) one -> p (t one)", p=P))
+        nc.sync.dma_start(offsets[:], offs)
         nc.sync.dma_start(windows[0][:], base[0:P, :])
+
+        primer = held.tile([P, 1], F32, name="primer")
+        primed = held.tile([P, 1], F32, name="primed")
+        nc.vector.memset(primer[:], 0.0)
+        nc.scalar.activation(primed[:], primer[:], IDENTITY)
         nc.scalar.dma_start(windows[1][:], base[P : 2 * P, :])
 
         fs_f32 = [held.tile([P, N], F32, name=f"fs_f32_{t}") for t in range(BLOCKS)]
@@ -67,5 +70,4 @@ def tile_dsvt_ort_kernel(tc, base, fs, w_v, b_v, w_o, b_o, offs, out):
             s2 = held.tile([P, N], F32, name=f"s2_{c}")
             nc.scalar.activation(s2[:], s2_acc[:], IDENTITY, bias=bo[:, c : c + 1])
             nc.vector.tensor_tensor(windows[c][:].indirect(offsets[:]), fs_f32[c][:], s2[:], ADD)
-            store_queue = nc.sync if c == 0 else nc.scalar
-            store_queue.dma_start(out[c * P : (c + 1) * P, :], windows[c][:])
+            nc.sync.dma_start(out[c * P : (c + 1) * P, :], windows[c][:])

@@ -10,8 +10,12 @@ ADD = mybir.AluOpType.add
 IDENTITY = mybir.ActivationFunctionType.Identity
 
 
-def by_block(matrix):
-    return matrix.rearrange("(t p) n -> p t n", p=P)
+def rows_interleaved(matrix):
+    return matrix.rearrange("(p t) n -> p t n", t=BLOCKS)
+
+
+def weights_interleaved(matrix):
+    return matrix.rearrange("(p t) (q u) -> p t q u", t=BLOCKS, u=BLOCKS)
 
 
 def tile_dsvt_ort_kernel(tc, base, fs, w_v, b_v, w_o, b_o, offs, out):
@@ -21,53 +25,52 @@ def tile_dsvt_ort_kernel(tc, base, fs, w_v, b_v, w_o, b_o, offs, out):
         tc.psum_pool(name="psum", bufs=1) as psum,
     ):
         fs_bf = held.tile([P, BLOCKS, N], BF16, name="fs_bf")
-        wv_bf = held.tile([P, BLOCKS, C], BF16, name="wv_bf")
-        wo_bf = held.tile([P, BLOCKS, C], BF16, name="wo_bf")
+        wv_bf = held.tile([P, BLOCKS, P, BLOCKS], BF16, name="wv_bf")
+        wo_bf = held.tile([P, BLOCKS, P, BLOCKS], BF16, name="wo_bf")
         bv = held.tile([P, BLOCKS], F32, name="bv")
         bo = held.tile([P, BLOCKS], F32, name="bo")
         offsets = held.tile([P, N // 16], U16, name="offsets")
         windows = [held.tile([P, S], F32, name=f"window{t}") for t in range(BLOCKS)]
 
-        nc.sync.dma_start(fs_bf[:], by_block(fs))
-        nc.sync.dma_start(wv_bf[:], by_block(w_v))
-        with nc.allow_non_contiguous_dma(reason="a bias: one float32 for each partition and block"):
-            nc.sync.dma_start(bv[:], b_v.rearrange("(t p) one -> p (t one)", p=P))
-            nc.sync.dma_start(wo_bf[:], by_block(w_o))
-            nc.sync.dma_start(bo[:], b_o.rearrange("(t p) one -> p (t one)", p=P))
+        nc.sync.dma_start(fs_bf[:], rows_interleaved(fs))
+        nc.scalar.dma_start(wv_bf[:], weights_interleaved(w_v))
+        nc.sync.dma_start(bv[:], rows_interleaved(b_v).rearrange("p t one -> p (t one)"))
+        nc.sync.dma_start(wo_bf[:], weights_interleaved(w_o))
+        nc.sync.dma_start(bo[:], rows_interleaved(b_o).rearrange("p t one -> p (t one)"))
         nc.sync.dma_start(offsets[:], offs)
-        nc.sync.dma_start(windows[0][:], base[0:P, :])
+        nc.scalar.dma_start(windows[0][:], rows_interleaved(base)[:, 0, :])
+        nc.sync.dma_start(windows[1][:], rows_interleaved(base)[:, 1, :])
 
         primer = held.tile([P, 1], F32, name="primer")
         primed = held.tile([P, 1], F32, name="primed")
         nc.vector.memset(primer[:], 0.0)
         nc.scalar.activation(primed[:], primer[:], IDENTITY)
-        nc.scalar.dma_start(windows[1][:], base[P : 2 * P, :])
 
         fs_f32 = [held.tile([P, N], F32, name=f"fs_f32_{t}") for t in range(BLOCKS)]
         for t in range(BLOCKS):
             nc.gpsimd.tensor_copy(fs_f32[t][:], fs_bf[:, t, :])
 
-        v_bf = [held.tile([P, N], BF16, name=f"v_bf{m}") for m in range(BLOCKS)]
-        for m in range(BLOCKS):
-            v_acc = psum.tile([P, N], F32, name=f"v_acc{m}")
-            for k in range(BLOCKS):
+        v_bf = [held.tile([P, N], BF16, name=f"v_bf{u}") for u in range(BLOCKS)]
+        for u in range(BLOCKS):
+            v_acc = psum.tile([P, N], F32, name=f"v_acc{u}")
+            for t in range(BLOCKS):
                 nc.tensor.matmul(
-                    v_acc[:], wv_bf[:, k, m * P : (m + 1) * P], fs_bf[:, k, :],
-                    start=(k == 0), stop=(k == BLOCKS - 1),
+                    v_acc[:], wv_bf[:, t, :, u], fs_bf[:, t, :],
+                    start=(t == 0), stop=(t == BLOCKS - 1),
                 )
-            if m == 0:
-                nc.vector.tensor_scalar(v_bf[m][:], v_acc[:], bv[:, m : m + 1], None, ADD)
+            if u == 0:
+                nc.vector.tensor_scalar(v_bf[u][:], v_acc[:], bv[:, u : u + 1], None, ADD)
             else:
-                nc.scalar.activation(v_bf[m][:], v_acc[:], IDENTITY, bias=bv[:, m : m + 1])
+                nc.scalar.activation(v_bf[u][:], v_acc[:], IDENTITY, bias=bv[:, u : u + 1])
 
-        for c in range(BLOCKS):
-            s2_acc = psum.tile([P, N], F32, name=f"s2_acc{c}")
-            for m in range(BLOCKS):
+        for t in range(BLOCKS):
+            s2_acc = psum.tile([P, N], F32, name=f"s2_acc{t}")
+            for u in range(BLOCKS):
                 nc.tensor.matmul(
-                    s2_acc[:], wo_bf[:, m, c * P : (c + 1) * P], v_bf[m][:],
-                    start=(m == 0), stop=(m == BLOCKS - 1),
+                    s2_acc[:], wo_bf[:, u, :, t], v_bf[u][:],
+                    start=(u == 0), stop=(u == BLOCKS - 1),
                 )
-            s2 = held.tile([P, N], F32, name=f"s2_{c}")
-            nc.scalar.activation(s2[:], s2_acc[:], IDENTITY, bias=bo[:, c : c + 1])
-            nc.vector.tensor_tensor(windows[c][:].indirect(offsets[:]), fs_f32[c][:], s2[:], ADD)
-            nc.sync.dma_start(out[c * P : (c + 1) * P, :], windows[c][:])
+            s2 = held.tile([P, N], F32, name=f"s2_{t}")
+            nc.scalar.activation(s2[:], s2_acc[:], IDENTITY, bias=bo[:, t : t + 1])
+            nc.vector.tensor_tensor(windows[t][:].indirect(offsets[:]), fs_f32[t][:], s2[:], ADD)
+            nc.sync.dma_start(rows_interleaved(out)[:, t, :], windows[t][:])

@@ -5,6 +5,9 @@ C, S, N = 256, 1024, 256
 BLOCKS = C // P
 FLOPS = 2 * (2 * C * C * N)
 
+WARM_COLUMNS = 512
+WARM_MATMULS = 4
+
 BF16, F32, U16 = mybir.dt.bfloat16, mybir.dt.float32, mybir.dt.uint16
 ADD = mybir.AluOpType.add
 IDENTITY = mybir.ActivationFunctionType.Identity
@@ -41,10 +44,13 @@ def tile_dsvt_ort_kernel(tc, base, fs, w_v, b_v, w_o, b_o, offs, out):
         nc.scalar.dma_start(windows[0][:], rows_interleaved(base)[:, 0, :])
         nc.sync.dma_start(windows[1][:], rows_interleaved(base)[:, 1, :])
 
-        primer = held.tile([P, 1], F32, name="primer")
+        zeros = held.tile([P, WARM_COLUMNS], BF16, name="zeros")
+        nc.vector.memset(zeros[:], 0.0)
         primed = held.tile([P, 1], F32, name="primed")
-        nc.vector.memset(primer[:], 0.0)
-        nc.scalar.activation(primed[:], primer[:], IDENTITY)
+        nc.scalar.activation(primed[:], zeros[:, 0:1], IDENTITY)
+        warm_acc = psum.tile([P, WARM_COLUMNS], F32, name="warm_acc")
+        for i in range(WARM_MATMULS):
+            nc.tensor.matmul(warm_acc[:], zeros[:, 0:P], zeros[:], start=True, stop=True)
 
         fs_f32 = [held.tile([P, N], F32, name=f"fs_f32_{t}") for t in range(BLOCKS)]
         for t in range(BLOCKS):

@@ -5,8 +5,7 @@ C, S, N = 256, 1024, 256
 BLOCKS = C // P
 FLOPS = 2 * (2 * C * C * N)
 
-WARM_COLUMNS = 512
-WARM_MATMULS = 4
+WARM_MATMULS = 14
 
 BF16, F32, U16 = mybir.dt.bfloat16, mybir.dt.float32, mybir.dt.uint16
 ADD = mybir.AluOpType.add
@@ -44,13 +43,13 @@ def tile_dsvt_ort_kernel(tc, base, fs, w_v, b_v, w_o, b_o, offs, out):
         nc.scalar.dma_start(windows[0][:], rows_interleaved(base)[:, 0, :])
         nc.sync.dma_start(windows[1][:], rows_interleaved(base)[:, 1, :])
 
-        zeros = held.tile([P, WARM_COLUMNS], BF16, name="zeros")
+        zeros = held.tile([P, P], BF16, name="zeros")
         nc.vector.memset(zeros[:], 0.0)
         primed = held.tile([P, 1], F32, name="primed")
         nc.scalar.activation(primed[:], zeros[:, 0:1], IDENTITY)
-        warm_acc = psum.tile([P, WARM_COLUMNS], F32, name="warm_acc")
+        warm_acc = psum.tile([P, P], F32, name="warm_acc")
         for i in range(WARM_MATMULS):
-            nc.tensor.matmul(warm_acc[:], zeros[:, 0:P], zeros[:], start=True, stop=True)
+            nc.tensor.matmul(warm_acc[:], zeros[:], zeros[:], start=True, stop=True)
 
         fs_f32 = [held.tile([P, N], F32, name=f"fs_f32_{t}") for t in range(BLOCKS)]
         for t in range(BLOCKS):

@@ -3,6 +3,9 @@ import concourse.mybir as mybir
 P = 128
 C, S, N = 256, 1024, 256
 BLOCKS = C // P
+HALVES = 2
+HALF = N // HALVES
+PSUM_BANKS = 8
 FLOPS = 2 * (2 * C * C * N)
 
 WARM_MATMULS = 14
@@ -24,7 +27,7 @@ def tile_dsvt_ort_kernel(tc, base, fs, w_v, b_v, w_o, b_o, offs, out):
     nc = tc.nc
     with (
         tc.tile_pool(name="held", bufs=1) as held,
-        tc.psum_pool(name="psum", bufs=1) as psum,
+        tc.psum_pool(name="psum", bufs=PSUM_BANKS) as psum,
     ):
         fs_bf = held.tile([P, BLOCKS, N], BF16, name="fs_bf")
         wv_bf = held.tile([P, BLOCKS, P, BLOCKS], BF16, name="wv_bf")
@@ -36,18 +39,16 @@ def tile_dsvt_ort_kernel(tc, base, fs, w_v, b_v, w_o, b_o, offs, out):
 
         nc.sync.dma_start(fs_bf[:], rows_interleaved(fs))
         nc.scalar.dma_start(wv_bf[:], weights_interleaved(w_v))
+        nc.gpsimd.dma_start(windows[1][:], rows_interleaved(base)[:, 1, :])
         nc.sync.dma_start(bv[:], rows_interleaved(b_v).rearrange("p t one -> p (t one)"))
+        nc.scalar.dma_start(windows[0][:], rows_interleaved(base)[:, 0, :])
         nc.sync.dma_start(wo_bf[:], weights_interleaved(w_o))
         nc.sync.dma_start(bo[:], rows_interleaved(b_o).rearrange("p t one -> p (t one)"))
         nc.sync.dma_start(offsets[:], offs)
-        nc.scalar.dma_start(windows[0][:], rows_interleaved(base)[:, 0, :])
-        nc.sync.dma_start(windows[1][:], rows_interleaved(base)[:, 1, :])
 
         zeros = held.tile([P, P], BF16, name="zeros")
+        warm_acc = psum.tile([P, P], F32, name="warm_acc", tag="acc")
         nc.vector.memset(zeros[:], 0.0)
-        primed = held.tile([P, 1], F32, name="primed")
-        nc.scalar.activation(primed[:], zeros[:, 0:1], IDENTITY)
-        warm_acc = psum.tile([P, P], F32, name="warm_acc")
         for i in range(WARM_MATMULS):
             nc.tensor.matmul(warm_acc[:], zeros[:], zeros[:], start=True, stop=True)
 
@@ -55,27 +56,36 @@ def tile_dsvt_ort_kernel(tc, base, fs, w_v, b_v, w_o, b_o, offs, out):
         for t in range(BLOCKS):
             nc.gpsimd.tensor_copy(fs_f32[t][:], fs_bf[:, t, :])
 
+
         v_bf = [held.tile([P, N], BF16, name=f"v_bf{u}") for u in range(BLOCKS)]
-        for u in range(BLOCKS):
-            v_acc = psum.tile([P, N], F32, name=f"v_acc{u}")
-            for t in range(BLOCKS):
-                nc.tensor.matmul(
-                    v_acc[:], wv_bf[:, t, :, u], fs_bf[:, t, :],
-                    start=(t == 0), stop=(t == BLOCKS - 1),
+        for h in range(HALVES):
+            for u in range(BLOCKS):
+                v_acc = psum.tile([P, HALF], F32, name="v_acc", tag="acc")
+                for t in range(BLOCKS):
+                    nc.tensor.matmul(
+                        v_acc[:], wv_bf[:, t, :, u], fs_bf[:, t, h * HALF : (h + 1) * HALF],
+                        start=(t == 0), stop=(t == BLOCKS - 1),
+                    )
+                nc.vector.tensor_scalar(
+                    v_bf[u][:, h * HALF : (h + 1) * HALF], v_acc[:], bv[:, u : u + 1], None, ADD
                 )
-            if u == 0:
-                nc.vector.tensor_scalar(v_bf[u][:], v_acc[:], bv[:, u : u + 1], None, ADD)
-            else:
-                nc.scalar.activation(v_bf[u][:], v_acc[:], IDENTITY, bias=bv[:, u : u + 1])
 
         for t in range(BLOCKS):
-            s2_acc = psum.tile([P, N], F32, name=f"s2_acc{t}")
-            for u in range(BLOCKS):
-                nc.tensor.matmul(
-                    s2_acc[:], wo_bf[:, u, :, t], v_bf[u][:],
-                    start=(u == 0), stop=(u == BLOCKS - 1),
-                )
             s2 = held.tile([P, N], F32, name=f"s2_{t}")
-            nc.scalar.activation(s2[:], s2_acc[:], IDENTITY, bias=bo[:, t : t + 1])
+            for h in range(HALVES):
+                s2_acc = psum.tile([P, HALF], F32, name="s2_acc", tag="acc")
+                for u in range(BLOCKS):
+                    nc.tensor.matmul(
+                        s2_acc[:], wo_bf[:, u, :, t], v_bf[u][:, h * HALF : (h + 1) * HALF],
+                        start=(u == 0), stop=(u == BLOCKS - 1),
+                    )
+                if t == 0:
+                    nc.vector.tensor_scalar(
+                        s2[:, h * HALF : (h + 1) * HALF], s2_acc[:], bo[:, t : t + 1], None, ADD
+                    )
+                else:
+                    nc.scalar.activation(
+                        s2[:, h * HALF : (h + 1) * HALF], s2_acc[:], IDENTITY, bias=bo[:, t : t + 1]
+                    )
             nc.vector.tensor_tensor(windows[t][:].indirect(offsets[:]), fs_f32[t][:], s2[:], ADD)
             nc.sync.dma_start(rows_interleaved(out)[:, t, :], windows[t][:])

@@ -39,18 +39,20 @@ def tile_dsvt_ort_kernel(tc, base, fs, w_v, b_v, w_o, b_o, offs, out):
 
         nc.sync.dma_start(fs_bf[:], rows_interleaved(fs))
         nc.scalar.dma_start(wv_bf[:], weights_interleaved(w_v))
-        nc.gpsimd.dma_start(windows[1][:], rows_interleaved(base)[:, 1, :])
         nc.sync.dma_start(bv[:], rows_interleaved(b_v).rearrange("p t one -> p (t one)"))
         nc.scalar.dma_start(windows[0][:], rows_interleaved(base)[:, 0, :])
         nc.sync.dma_start(wo_bf[:], weights_interleaved(w_o))
         nc.sync.dma_start(bo[:], rows_interleaved(b_o).rearrange("p t one -> p (t one)"))
         nc.sync.dma_start(offsets[:], offs)
+        nc.sync.dma_start(windows[1][:], rows_interleaved(base)[:, 1, :])
 
         zeros = held.tile([P, P], BF16, name="zeros")
-        warm_acc = psum.tile([P, P], F32, name="warm_acc", tag="acc")
         nc.vector.memset(zeros[:], 0.0)
+        warm_acc = psum.tile([P, P], F32, name="warm_acc", tag="acc")
         for i in range(WARM_MATMULS):
             nc.tensor.matmul(warm_acc[:], zeros[:], zeros[:], start=True, stop=True)
+        primed = held.tile([P, 1], F32, name="primed")
+        nc.scalar.activation(primed[:], zeros[:, 0:1], IDENTITY)
 
         fs_f32 = [held.tile([P, N], F32, name=f"fs_f32_{t}") for t in range(BLOCKS)]
         for t in range(BLOCKS):

@@ -29,21 +29,23 @@ def tile_dsvt_ort_kernel(tc, base, fs, w_v, b_v, w_o, b_o, offs, out):
         tc.tile_pool(name="held", bufs=1) as held,
         tc.psum_pool(name="psum", bufs=PSUM_BANKS) as psum,
     ):
-        fs_bf = held.tile([P, BLOCKS, N], BF16, name="fs_bf")
-        wv_bf = held.tile([P, BLOCKS, P, BLOCKS], BF16, name="wv_bf")
+        fs_bf = [held.tile([P, N], BF16, name=f"fs_bf{t}") for t in range(BLOCKS)]
+        wv_bf = [held.tile([P, P, BLOCKS], BF16, name=f"wv_bf{t}") for t in range(BLOCKS)]
         wo_bf = held.tile([P, BLOCKS, P, BLOCKS], BF16, name="wo_bf")
         bv = held.tile([P, BLOCKS], F32, name="bv")
         bo = held.tile([P, BLOCKS], F32, name="bo")
         offsets = held.tile([P, N // 16], U16, name="offsets")
         windows = [held.tile([P, S], F32, name=f"window{t}") for t in range(BLOCKS)]
 
-        nc.sync.dma_start(fs_bf[:], rows_interleaved(fs))
-        nc.scalar.dma_start(wv_bf[:], weights_interleaved(w_v))
+        for t in range(BLOCKS):
+            nc.sync.dma_start(fs_bf[t][:], rows_interleaved(fs)[:, t, :])
+            nc.scalar.dma_start(wv_bf[t][:], weights_interleaved(w_v)[:, t, :, :])
         nc.sync.dma_start(bv[:], rows_interleaved(b_v).rearrange("p t one -> p (t one)"))
-        nc.scalar.dma_start(windows[0][:], rows_interleaved(base)[:, 0, :])
+        nc.scalar.dma_start(windows[0][:, : S // 2], rows_interleaved(base)[:, 0, : S // 2])
         nc.sync.dma_start(wo_bf[:], weights_interleaved(w_o))
         nc.sync.dma_start(bo[:], rows_interleaved(b_o).rearrange("p t one -> p (t one)"))
         nc.sync.dma_start(offsets[:], offs)
+        nc.sync.dma_start(windows[0][:, S // 2 :], rows_interleaved(base)[:, 0, S // 2 :])
         nc.sync.dma_start(windows[1][:], rows_interleaved(base)[:, 1, :])
 
         zeros = held.tile([P, P], BF16, name="zeros")
@@ -56,21 +58,22 @@ def tile_dsvt_ort_kernel(tc, base, fs, w_v, b_v, w_o, b_o, offs, out):
 
         fs_f32 = [held.tile([P, N], F32, name=f"fs_f32_{t}") for t in range(BLOCKS)]
         for t in range(BLOCKS):
-            nc.gpsimd.tensor_copy(fs_f32[t][:], fs_bf[:, t, :])
+            nc.gpsimd.tensor_copy(fs_f32[t][:], fs_bf[t][:])
 
 
         v_bf = [held.tile([P, N], BF16, name=f"v_bf{u}") for u in range(BLOCKS)]
-        for h in range(HALVES):
-            for u in range(BLOCKS):
-                v_acc = psum.tile([P, HALF], F32, name="v_acc", tag="acc")
-                for t in range(BLOCKS):
-                    nc.tensor.matmul(
-                        v_acc[:], wv_bf[:, t, :, u], fs_bf[:, t, h * HALF : (h + 1) * HALF],
-                        start=(t == 0), stop=(t == BLOCKS - 1),
-                    )
-                nc.vector.tensor_scalar(
-                    v_bf[u][:, h * HALF : (h + 1) * HALF], v_acc[:], bv[:, u : u + 1], None, ADD
+        pieces = [(h, u) for h in range(HALVES) for u in range(BLOCKS)]
+        v_acc = {piece: psum.tile([P, HALF], F32, name="v_acc", tag="acc") for piece in pieces}
+        for t in range(BLOCKS):
+            for h, u in pieces:
+                nc.tensor.matmul(
+                    v_acc[(h, u)][:], wv_bf[t][:, :, u], fs_bf[t][:, h * HALF : (h + 1) * HALF],
+                    start=(t == 0), stop=(t == BLOCKS - 1),
                 )
+        for h, u in pieces:
+            nc.vector.tensor_scalar(
+                v_bf[u][:, h * HALF : (h + 1) * HALF], v_acc[(h, u)][:], bv[:, u : u + 1], None, ADD
+            )
 
         for t in range(BLOCKS):
             s2 = held.tile([P, N], F32, name=f"s2_{t}")

@@ -8,7 +8,7 @@ HALF = N // HALVES
 PSUM_BANKS = 8
 FLOPS = 2 * (2 * C * C * N)
 
-WARM_MATMULS = 14
+WARM_MATMULS = 10
 
 BF16, F32, U16 = mybir.dt.bfloat16, mybir.dt.float32, mybir.dt.uint16
 ADD = mybir.AluOpType.add

@@ -71,9 +71,14 @@ def tile_dsvt_ort_kernel(tc, base, fs, w_v, b_v, w_o, b_o, offs, out):
                     start=(t == 0), stop=(t == BLOCKS - 1),
                 )
         for h, u in pieces:
-            nc.vector.tensor_scalar(
-                v_bf[u][:, h * HALF : (h + 1) * HALF], v_acc[(h, u)][:], bv[:, u : u + 1], None, ADD
-            )
+            if u == 0:
+                nc.vector.tensor_scalar(
+                    v_bf[u][:, h * HALF : (h + 1) * HALF], v_acc[(h, u)][:], bv[:, u : u + 1], None, ADD
+                )
+            else:
+                nc.scalar.activation(
+                    v_bf[u][:, h * HALF : (h + 1) * HALF], v_acc[(h, u)][:], IDENTITY, bias=bv[:, u : u + 1]
+                )
 
         for t in range(BLOCKS):
             s2 = held.tile([P, N], F32, name=f"s2_{t}")

@@ -57,8 +57,7 @@ def tile_dsvt_ort_kernel(tc, base, fs, w_v, b_v, w_o, b_o, offs, out):
         nc.scalar.activation(primed[:], zeros[:, 0:1], IDENTITY)
 
         fs_f32 = [held.tile([P, N], F32, name=f"fs_f32_{t}") for t in range(BLOCKS)]
-        for t in range(BLOCKS):
-            nc.gpsimd.tensor_copy(fs_f32[t][:], fs_bf[t][:])
+        nc.vector.tensor_copy(fs_f32[0][:], fs_bf[0][:])
 
 
         v_bf = [held.tile([P, N], BF16, name=f"v_bf{u}") for u in range(BLOCKS)]
@@ -79,6 +78,7 @@ def tile_dsvt_ort_kernel(tc, base, fs, w_v, b_v, w_o, b_o, offs, out):
                 nc.scalar.activation(
                     v_bf[u][:, h * HALF : (h + 1) * HALF], v_acc[(h, u)][:], IDENTITY, bias=bv[:, u : u + 1]
                 )
+        nc.scalar.activation(fs_f32[1][:], fs_bf[1][:], IDENTITY)
 
         for t in range(BLOCKS):
             s2 = held.tile([P, N], F32, name=f"s2_{t}")

@@ -3,7 +3,7 @@ import concourse.mybir as mybir
 P = 128
 C, S, N = 256, 1024, 256
 BLOCKS = C // P
-HALVES = 2
+HALVES = 4
 HALF = N // HALVES
 PSUM_BANKS = 8
 FLOPS = 2 * (2 * C * C * N)

@@ -41,11 +41,10 @@ def tile_dsvt_ort_kernel(tc, base, fs, w_v, b_v, w_o, b_o, offs, out):
             nc.sync.dma_start(fs_bf[t][:], rows_interleaved(fs)[:, t, :])
             nc.scalar.dma_start(wv_bf[t][:], weights_interleaved(w_v)[:, t, :, :])
         nc.sync.dma_start(bv[:], rows_interleaved(b_v).rearrange("p t one -> p (t one)"))
-        nc.scalar.dma_start(windows[0][:, : S // 2], rows_interleaved(base)[:, 0, : S // 2])
         nc.sync.dma_start(wo_bf[:], weights_interleaved(w_o))
         nc.sync.dma_start(bo[:], rows_interleaved(b_o).rearrange("p t one -> p (t one)"))
+        nc.sync.dma_start(windows[0][:], rows_interleaved(base)[:, 0, :])
         nc.sync.dma_start(offsets[:], offs)
-        nc.sync.dma_start(windows[0][:, S // 2 :], rows_interleaved(base)[:, 0, S // 2 :])
         nc.sync.dma_start(windows[1][:], rows_interleaved(base)[:, 1, :])
 
         zeros = held.tile([P, P], BF16, name="zeros")

import concourse.mybir as mybir

P = 128
C, S, N = 256, 1024, 256
BLOCKS = C // P
HALVES = 4
HALF = N // HALVES
PSUM_BANKS = 8
FLOPS = 2 * (2 * C * C * N)

WARM_MATMULS = 10

BF16, F32, U16 = mybir.dt.bfloat16, mybir.dt.float32, mybir.dt.uint16
ADD = mybir.AluOpType.add
IDENTITY = mybir.ActivationFunctionType.Identity


def rows_interleaved(matrix):
    return matrix.rearrange("(p t) n -> p t n", t=BLOCKS)


def weights_interleaved(matrix):
    return matrix.rearrange("(p t) (q u) -> p t q u", t=BLOCKS, u=BLOCKS)


def tile_dsvt_ort_kernel(tc, base, fs, w_v, b_v, w_o, b_o, offs, out):
    nc = tc.nc
    with (
        tc.tile_pool(name="held", bufs=1) as held,
        tc.psum_pool(name="psum", bufs=PSUM_BANKS) as psum,
    ):
        fs_bf = [held.tile([P, N], BF16, name=f"fs_bf{t}") for t in range(BLOCKS)]
        wv_bf = [held.tile([P, P, BLOCKS], BF16, name=f"wv_bf{t}") for t in range(BLOCKS)]
        wo_bf = held.tile([P, BLOCKS, P, BLOCKS], BF16, name="wo_bf")
        bv = held.tile([P, BLOCKS], F32, name="bv")
        bo = held.tile([P, BLOCKS], F32, name="bo")
        offsets = held.tile([P, N // 16], U16, name="offsets")
        windows = [held.tile([P, S], F32, name=f"window{t}") for t in range(BLOCKS)]

        for t in range(BLOCKS):
            nc.sync.dma_start(fs_bf[t][:], rows_interleaved(fs)[:, t, :])
            nc.scalar.dma_start(wv_bf[t][:], weights_interleaved(w_v)[:, t, :, :])
        nc.sync.dma_start(bv[:], rows_interleaved(b_v).rearrange("p t one -> p (t one)"))
        nc.sync.dma_start(wo_bf[:], weights_interleaved(w_o))
        nc.sync.dma_start(bo[:], rows_interleaved(b_o).rearrange("p t one -> p (t one)"))
        nc.sync.dma_start(windows[0][:], rows_interleaved(base)[:, 0, :])
        nc.sync.dma_start(offsets[:], offs)
        nc.sync.dma_start(windows[1][:], rows_interleaved(base)[:, 1, :])

        zeros = held.tile([P, P], BF16, name="zeros")
        nc.vector.memset(zeros[:], 0.0)
        warm_acc = psum.tile([P, P], F32, name="warm_acc", tag="acc")
        for i in range(WARM_MATMULS):
            nc.tensor.matmul(warm_acc[:], zeros[:], zeros[:], start=True, stop=True)
        primed = held.tile([P, 1], F32, name="primed")
        nc.scalar.activation(primed[:], zeros[:, 0:1], IDENTITY)

        fs_f32 = [held.tile([P, N], F32, name=f"fs_f32_{t}") for t in range(BLOCKS)]
        nc.vector.tensor_copy(fs_f32[0][:], fs_bf[0][:])


        v_bf = [held.tile([P, N], BF16, name=f"v_bf{u}") for u in range(BLOCKS)]
        pieces = [(h, u) for h in range(HALVES) for u in range(BLOCKS)]
        v_acc = {piece: psum.tile([P, HALF], F32, name="v_acc", tag="acc") for piece in pieces}
        for t in range(BLOCKS):
            for h, u in pieces:
                nc.tensor.matmul(
                    v_acc[(h, u)][:], wv_bf[t][:, :, u], fs_bf[t][:, h * HALF : (h + 1) * HALF],
                    start=(t == 0), stop=(t == BLOCKS - 1),
                )
        for h, u in pieces:
            if u == 0:
                nc.vector.tensor_scalar(
                    v_bf[u][:, h * HALF : (h + 1) * HALF], v_acc[(h, u)][:], bv[:, u : u + 1], None, ADD
                )
            else:
                nc.scalar.activation(
                    v_bf[u][:, h * HALF : (h + 1) * HALF], v_acc[(h, u)][:], IDENTITY, bias=bv[:, u : u + 1]
                )
        nc.scalar.activation(fs_f32[1][:], fs_bf[1][:], IDENTITY)

        for t in range(BLOCKS):
            s2 = held.tile([P, N], F32, name=f"s2_{t}")
            for h in range(HALVES):
                s2_acc = psum.tile([P, HALF], F32, name="s2_acc", tag="acc")
                for u in range(BLOCKS):
                    nc.tensor.matmul(
                        s2_acc[:], wo_bf[:, u, :, t], v_bf[u][:, h * HALF : (h + 1) * HALF],
                        start=(u == 0), stop=(u == BLOCKS - 1),
                    )
                if t == 0:
                    nc.vector.tensor_scalar(
                        s2[:, h * HALF : (h + 1) * HALF], s2_acc[:], bo[:, t : t + 1], None, ADD
                    )
                else:
                    nc.scalar.activation(
                        s2[:, h * HALF : (h + 1) * HALF], s2_acc[:], IDENTITY, bias=bo[:, t : t + 1]
                    )
            nc.vector.tensor_tensor(windows[t][:].indirect(offsets[:]), fs_f32[t][:], s2[:], ADD)
            nc.sync.dma_start(rows_interleaved(out)[:, t, :], windows[t][:])
